import numpy as np
import ml_dtypes


def mxq(x, axis, fmt="e4m3"):
    dtype, down = {"e4m3": (ml_dtypes.float8_e4m3fn, 7), "e5m2": (ml_dtypes.float8_e5m2, 14)}[fmt]
    v = np.moveaxis(np.asarray(x, np.float32).astype(ml_dtypes.bfloat16).astype(np.float64), axis, -1)
    blocks = v.reshape(v.shape[:-1] + (-1, 32))
    amax = np.abs(blocks).max(-1, keepdims=True)
    byte = np.maximum(np.where(amax > 0, np.frexp(amax)[1] - 1 + 127, 0) - down, 1)
    scale = np.exp2(byte - 127.0)
    codes = (blocks / scale).astype(np.float32).astype(dtype).astype(np.float64)
    return np.moveaxis((codes * scale).reshape(v.shape), -1, axis)


WIDE = False


def mx_kscale(k):
    if not WIDE:
        return np.ones(k)
    levels = np.array([10, -10, 5, -5, 0])
    a = np.random.permutation(np.resize(levels, k // 512 * 4)).reshape(k // 512, 4)
    idx = np.arange(k)
    return np.exp2(a[idx // 512, idx % 128 // 32])


BF16 = ml_dtypes.bfloat16


def bf(x):
    return np.asarray(x, np.float32).astype(BF16)


def f64(x):
    return np.asarray(x).astype(np.float64)


B, LC, LL, LLAMA_DIM, DIM, HEADS, FF = 4, 77, 64, 2048, 1536, 16, 6144
EPS = 1e-5


def layernorm(x, g, b):
    m = x.mean(-1, keepdims=True)
    v = ((x - m) ** 2).mean(-1, keepdims=True)
    return (x - m) / np.sqrt(v + EPS) * g + b


def setup_inputs():
    s, t = mx_kscale(LLAMA_DIM), mx_kscale(DIM)
    return {
        "llm_embed": bf(np.random.standard_normal((B, LL, LLAMA_DIM)) * s),
        "llm_proj_w": bf(np.random.standard_normal((DIM, LLAMA_DIM)) / np.sqrt(LLAMA_DIM) / s),
        "llm_proj_b": bf(0.1 * np.random.standard_normal(DIM)),
        "kvn_g": bf((1.0 + 0.1 * np.random.standard_normal(DIM)) * t),
        "kvn_b": bf(0.1 * np.random.standard_normal(DIM) * t),
        "q_w": bf(np.random.standard_normal((DIM, DIM)) / np.sqrt(DIM) / t),
        "q_b": bf(0.1 * np.random.standard_normal(DIM)),
    }


def reference(llm_embed, llm_proj_w, llm_proj_b, kvn_g, kvn_b, q_w, q_b):
    llm = (mxq(f64(llm_embed), 2, "e4m3") @ mxq(f64(llm_proj_w), 1, "e4m3").T) + f64(llm_proj_b)
    llm_n = layernorm(llm, f64(kvn_g), f64(kvn_b))
    q = (mxq(llm_n, 2, "e4m3") @ mxq(f64(q_w), 1, "e4m3").T) + f64(q_b)
    return llm, q

@@ -1,0 +1,244 @@
+import concourse.mybir as mybir
+from concourse.masks import make_identity
+
+F32 = mybir.dt.float32
+BF16 = mybir.dt.bfloat16
+U32 = mybir.dt.uint32
+U8 = mybir.dt.uint8
+I32 = mybir.dt.int32
+FP8X4 = mybir.dt.float8_e4m3fn_x4
+ALU = mybir.AluOpType
+ACT = mybir.ActivationFunctionType
+
+P = 128
+PACK = 4
+K_PASS = P * PACK
+ROWS = 2 * P
+TOKENS = 256
+TOKEN_TILES = TOKENS // P
+K1 = 2048
+DIM = 1536
+PASSES1 = K1 // K_PASS
+PASSES2 = DIM // K_PASS
+UNITS = DIM // ROWS
+BANK = 512
+CHUNKS = DIM // BANK
+EPS = 1e-5
+
+FLOPS = 2 * TOKENS * K1 * DIM + 2 * TOKENS * DIM * DIM
+
+
+def tile_crossfusion_pa_kernel(
+    tc, llm_embed, llm_proj_w, llm_proj_b, kvn_g, kvn_b, q_w, q_b, out_0, out_1
+):
+    nc = tc.nc
+    x_rows = llm_embed.flatten_outer_dims()
+    llm_out = out_0.flatten_outer_dims()
+    q_out = out_1.flatten_outer_dims()
+
+    with tc.tile_pool(name="keep", bufs=1) as keep, tc.tile_pool(
+        name="stage", bufs=6
+    ) as stage, tc.tile_pool(name="w1q", bufs=3) as w1q, tc.psum_pool(
+        name="psum", bufs=8
+    ) as psum, tc.manual_schedule():
+
+        def load_unit(rows, width, name):
+            raw = keep.tile([P, 2, width], BF16, name=name)
+            nc.sync.dma_start(out=raw[:], in_=rows.rearrange("(r p) k -> p r k", p=P))
+            return raw
+
+        bias_rows = keep.tile([P, 2 * DIM], BF16)
+        nc.vector.memset(bias_rows[:].bitcast(I32), 0)
+        gb_rows = keep.tile([P, 2 * P], BF16)
+        nc.vector.memset(gb_rows[:].bitcast(I32), 0)
+        ones = keep.tile([P, P], BF16)
+        nc.vector.memset(ones[:], 1.0)
+        eps = keep.tile([P, 1], F32)
+        nc.vector.memset(eps[:], EPS)
+        ident = keep.tile([P, P], F32)
+        make_identity(nc, ident[:])
+
+        warm = keep.tile([P, 1], F32)
+        nc.scalar.activation(out=warm[:], in_=eps[:], func=ACT.Sqrt)
+
+        x_raw = load_unit(x_rows, K1, "x_raw")
+        nc.sync.dma_start(out=bias_rows[0:1, 0:DIM], in_=llm_proj_b.rearrange("(o n) -> o n", o=1))
+        nc.sync.dma_start(out=bias_rows[0:1, DIM : 2 * DIM], in_=q_b.rearrange("(o n) -> o n", o=1))
+        nc.sync.dma_start(out=gb_rows[0:UNITS, :], in_=kvn_g.rearrange("(b w) -> b w", w=ROWS))
+        nc.sync.dma_start(out=gb_rows[UNITS : 2 * UNITS, :], in_=kvn_b.rearrange("(b w) -> b w", w=ROWS))
+        w1_raw = [load_unit(llm_proj_w[u * ROWS : (u + 1) * ROWS, :], K1, "w1_raw%d" % u) for u in range(UNITS)]
+        w2_raw = [load_unit(q_w[u * ROWS : (u + 1) * ROWS, :], DIM, "w2_raw%d" % u) for u in range(UNITS)]
+
+        def transpose_unit(raw, passes):
+            grouped_tiles = []
+            for g in range(passes):
+                bank = psum.tile([P, 2, ROWS], F32, tag="bank", name="bank")
+                for u in range(2):
+                    first = (2 * g + u) * P
+                    for r in range(2):
+                        nc.tensor.transpose(
+                            bank[:, u, r * P : (r + 1) * P],
+                            raw[:, r, :].bitcast(F32)[:, first : first + P],
+                            ident[:],
+                        )
+                grouped = stage.tile([P, ROWS * PACK], BF16, align_bytes=64, tag="grouped", name="grouped")
+                nc.scalar.copy(
+                    out=grouped[:].bitcast(F32).rearrange("p (c u) -> p c u", u=2),
+                    in_=bank[:].rearrange("p u c -> p c u"),
+                )
+                grouped_tiles.append(grouped)
+            return grouped_tiles
+
+        def quantise_unit(grouped_tiles, codes, scales, cols):
+            for g, grouped in enumerate(grouped_tiles):
+                nc.vector.quantize_mx(
+                    out=codes[:, g, cols].bitcast(FP8X4), scales=scales[:, g, cols], in_=grouped[:]
+                )
+
+        x_codes = keep.tile([P, PASSES1, TOKENS], U32, align_bytes=64)
+        x_scales = keep.tile([P, PASSES1, TOKENS], U8, align_bytes=64)
+        w2_codes = keep.tile([P, PASSES2, DIM], U32, align_bytes=64)
+        w2_scales = keep.tile([P, PASSES2, DIM], U8, align_bytes=64)
+        llm = keep.tile([P, TOKEN_TILES, DIM], F32)
+        stats = keep.tile([P, TOKEN_TILES, UNITS, 6], F32)
+
+        def first_matmul(u, w1_codes, w1_scales):
+            acc = psum.tile([P, TOKEN_TILES, ROWS], F32, tag="bank", name="acc")
+            for i in range(TOKEN_TILES):
+                tokens = slice(i * P, (i + 1) * P)
+                for g in range(PASSES1):
+                    nc.tensor.matmul_mx(
+                        out=acc[:, i, :],
+                        lhsT=x_codes[:, g, tokens].bitcast(FP8X4),
+                        lhsT_scale=x_scales[:, g, tokens],
+                        rhs=w1_codes[:, g, :].bitcast(FP8X4),
+                        rhs_scale=w1_scales[:, g, :],
+                        start=(g == 0),
+                        stop=(g == PASSES1 - 1),
+                    )
+            cols = slice(u * ROWS, (u + 1) * ROWS)
+            nc.vector.tensor_tensor(
+                out=llm[:, :, cols],
+                in0=acc[:],
+                in1=bias_all[:, cols].unsqueeze(1).to_broadcast([P, TOKEN_TILES, ROWS]),
+                op=ALU.add,
+            )
+            for i in range(TOKEN_TILES):
+                nc.vector.bn_stats(out=stats[:, i, u, :], in_=llm[:, i, cols])
+
+        def quantise_w1(grouped_tiles):
+            w1_codes = w1q.tile([P, PASSES1, ROWS], U32, align_bytes=64, name="w1_codes")
+            w1_scales = w1q.tile([P, PASSES1, ROWS], U8, align_bytes=64, name="w1_scales")
+            quantise_unit(grouped_tiles, w1_codes, w1_scales, slice(0, ROWS))
+            return w1_codes, w1_scales
+
+        def quantise_w2(u, grouped_tiles):
+            quantise_unit(grouped_tiles, w2_codes, w2_scales, slice(u * ROWS, (u + 1) * ROWS))
+
+        quantise_unit(transpose_unit(x_raw, PASSES1), x_codes, x_scales, slice(0, TOKENS))
+
+        bias_all = keep.tile([P, 2 * DIM], BF16)
+        for c in range(2 * CHUNKS):
+            bank = psum.tile([P, BANK], F32, tag="bank", name="bank")
+            nc.tensor.matmul(
+                out=bank[:], lhsT=ones[:], rhs=bias_rows[:, c * BANK : (c + 1) * BANK], start=True, stop=True
+            )
+            nc.vector.tensor_copy(out=bias_all[:, c * BANK : (c + 1) * BANK], in_=bank[:])
+        gb_bank = psum.tile([P, BANK], F32, tag="bank", name="bank")
+        nc.tensor.transpose(gb_bank[:, 0:P], gb_rows[:].bitcast(F32), ident[:])
+        gb_col = keep.tile([P, 2, UNITS, 2], F32)
+        nc.vector.tensor_copy(
+            out=gb_col[:].rearrange("p v b e -> p (v b e)"), in_=gb_bank[:, 0 : 2 * UNITS].bitcast(BF16)
+        )
+
+        ready = quantise_w1(transpose_unit(w1_raw[0], PASSES1))
+        for u in range(UNITS):
+            if u + 1 < UNITS:
+                following = transpose_unit(w1_raw[u + 1], PASSES1)
+            else:
+                following = transpose_unit(w2_raw[0], PASSES2)
+            first_matmul(u, ready[0], ready[1])
+            if u + 1 < UNITS:
+                ready = quantise_w1(following)
+            else:
+                quantise_w2(0, following)
+        for i in range(TOKEN_TILES):
+            nc.sync.dma_start(out=llm_out[i * P : (i + 1) * P, :], in_=llm[:, i, :])
+
+        w2_grouped = transpose_unit(w2_raw[1], PASSES2)
+        mean_var = keep.tile([P, TOKEN_TILES, 2], F32)
+        for i in range(TOKEN_TILES):
+            nc.vector.bn_aggr(out=mean_var[:, i, :], in_=stats[:, i, :, :].rearrange("p u s -> p (u s)"))
+        std = keep.tile([P, TOKEN_TILES], F32)
+        nc.scalar.activation(out=std[:], in_=mean_var[:, :, 1], func=ACT.Sqrt, bias=eps[:, 0:1], scale=1.0)
+        rstd = keep.tile([P, TOKEN_TILES], F32)
+        nc.vector.reciprocal(out=rstd[:], in_=std[:])
+        offset = keep.tile([P, TOKEN_TILES], F32)
+        nc.vector.scalar_tensor_tensor(
+            out=offset[:], in0=mean_var[:, :, 0], scalar=-1.0, in1=rstd[:], op0=ALU.mult, op1=ALU.mult
+        )
+        quantise_w2(1, w2_grouped)
+
+        xhat = keep.tile([P, TOKEN_TILES, UNITS, 2, P], F32)
+        n_codes = keep.tile([P, PASSES2, TOKENS], U32, align_bytes=64)
+        n_scales = keep.tile([P, PASSES2, TOKENS], U8, align_bytes=64)
+        for g in range(PASSES2):
+            for i in range(TOKEN_TILES):
+                source = llm[:, i, g * K_PASS : (g + 1) * K_PASS].rearrange("t (b p e) -> t b e p", b=2, e=2)
+                target = xhat[:, i, 2 * g : 2 * g + 2, :, :]
+                if i == 0:
+                    nc.vector.tensor_scalar(
+                        out=target, in0=source, scalar1=rstd[:, i : i + 1], scalar2=offset[:, i : i + 1],
+                        op0=ALU.mult, op1=ALU.add,
+                    )
+                else:
+                    nc.scalar.activation(
+                        out=target, in_=source, func=ACT.Identity, scale=rstd[:, i : i + 1], bias=offset[:, i : i + 1]
+                    )
+            planes = stage.tile([P, PACK, TOKENS], BF16, tag="planes", name="planes", bufs=2)
+            for u in range(2):
+                b = 2 * g + u
+                bank = psum.tile([P, 2, TOKENS], F32, tag="bank", name="bank")
+                for e in range(2):
+                    for i in range(TOKEN_TILES):
+                        nc.tensor.transpose(bank[:, e, i * P : (i + 1) * P], xhat[:, i, b, e, :], ident[:])
+                for e in range(2):
+                    nc.scalar.activation(
+                        out=planes[:, 2 * u + e, :], in_=bank[:, e, :], func=ACT.Identity,
+                        scale=gb_col[:, 0, b, e : e + 1], bias=gb_col[:, 1, b, e : e + 1],
+                    )
+            grouped = stage.tile([P, TOKENS * PACK], BF16, align_bytes=64, tag="grouped", name="grouped")
+            nc.vector.tensor_copy(
+                out=grouped[:].rearrange("p (r t) -> p r t", t=PACK), in_=planes[:].rearrange("p t r -> p r t")
+            )
+            w2_grouped = transpose_unit(w2_raw[2 + g], PASSES2)
+            nc.vector.quantize_mx(out=n_codes[:, g, :].bitcast(FP8X4), scales=n_scales[:, g, :], in_=grouped[:])
+            quantise_w2(2 + g, w2_grouped)
+        quantise_w2(5, transpose_unit(w2_raw[5], PASSES2))
+
+        q_sb = keep.tile([P, TOKEN_TILES, DIM], F32)
+        accs = {}
+        for g in range(PASSES2):
+            for i in range(TOKEN_TILES):
+                tokens = slice(i * P, (i + 1) * P)
+                for c in range(CHUNKS):
+                    cols = slice(c * BANK, (c + 1) * BANK)
+                    if g == 0:
+                        accs[(i, c)] = psum.tile([P, BANK], F32, tag="bank", name="acc")
+                    nc.tensor.matmul_mx(
+                        out=accs[(i, c)][:],
+                        lhsT=n_codes[:, g, tokens].bitcast(FP8X4),
+                        lhsT_scale=n_scales[:, g, tokens],
+                        rhs=w2_codes[:, g, cols].bitcast(FP8X4),
+                        rhs_scale=w2_scales[:, g, cols],
+                        start=(g == 0),
+                        stop=(g == PASSES2 - 1),
+                    )
+        for i in range(TOKEN_TILES):
+            for c in range(CHUNKS):
+                cols = slice(c * BANK, (c + 1) * BANK)
+                nc.vector.tensor_tensor(
+                    out=q_sb[:, i, cols], in0=accs[(i, c)][:], in1=bias_all[:, DIM + c * BANK : DIM + (c + 1) * BANK],
+                    op=ALU.add,
+                )
+                nc.sync.dma_start(out=q_out[i * P : (i + 1) * P, cols], in_=q_sb[:, i, cols])

@@ -47,8 +47,8 @@ def tile_crossfusion_pa_kernel(
             nc.sync.dma_start(out=raw[:], in_=rows.rearrange("(r p) k -> p r k", p=P))
             return raw
 
-        bias_rows = keep.tile([P, 2 * DIM], BF16)
-        nc.vector.memset(bias_rows[:].bitcast(I32), 0)
+        b1_rows = keep.tile([P, DIM], BF16)
+        nc.vector.memset(b1_rows[:].bitcast(I32), 0)
         gb_rows = keep.tile([P, 2 * P], BF16)
         nc.vector.memset(gb_rows[:].bitcast(I32), 0)
         ones = keep.tile([P, P], BF16)
@@ -57,17 +57,17 @@ def tile_crossfusion_pa_kernel(
         nc.vector.memset(eps[:], EPS)
         ident = keep.tile([P, P], F32)
         make_identity(nc, ident[:])
-
         warm = keep.tile([P, 1], F32)
         nc.scalar.activation(out=warm[:], in_=eps[:], func=ACT.Sqrt)
 
         x_raw = load_unit(x_rows, K1, "x_raw")
-        nc.sync.dma_start(out=bias_rows[0:1, 0:DIM], in_=llm_proj_b.rearrange("(o n) -> o n", o=1))
-        nc.sync.dma_start(out=bias_rows[0:1, DIM : 2 * DIM], in_=q_b.rearrange("(o n) -> o n", o=1))
+        nc.sync.dma_start(out=b1_rows[0:1, :], in_=llm_proj_b.rearrange("(o n) -> o n", o=1))
         nc.sync.dma_start(out=gb_rows[0:UNITS, :], in_=kvn_g.rearrange("(b w) -> b w", w=ROWS))
         nc.sync.dma_start(out=gb_rows[UNITS : 2 * UNITS, :], in_=kvn_b.rearrange("(b w) -> b w", w=ROWS))
         w1_raw = [load_unit(llm_proj_w[u * ROWS : (u + 1) * ROWS, :], K1, "w1_raw%d" % u) for u in range(UNITS)]
         w2_raw = [load_unit(q_w[u * ROWS : (u + 1) * ROWS, :], DIM, "w2_raw%d" % u) for u in range(UNITS)]
+        qb_all = keep.tile([P, DIM], BF16)
+        nc.sync.dma_start(out=qb_all[:], in_=q_b.partition_broadcast(P))
 
         def transpose_unit(raw, passes):
             grouped_tiles = []
@@ -99,8 +99,18 @@ def tile_crossfusion_pa_kernel(
         x_scales = keep.tile([P, PASSES1, TOKENS], U8, align_bytes=64)
         w2_codes = keep.tile([P, PASSES2, DIM], U32, align_bytes=64)
         w2_scales = keep.tile([P, PASSES2, DIM], U8, align_bytes=64)
+        b1_all = keep.tile([P, DIM], BF16)
         llm = keep.tile([P, TOKEN_TILES, DIM], F32)
         stats = keep.tile([P, TOKEN_TILES, UNITS, 6], F32)
+
+        def quantise_w1(grouped_tiles):
+            w1_codes = w1q.tile([P, PASSES1, ROWS], U32, align_bytes=64, name="w1_codes")
+            w1_scales = w1q.tile([P, PASSES1, ROWS], U8, align_bytes=64, name="w1_scales")
+            quantise_unit(grouped_tiles, w1_codes, w1_scales, slice(0, ROWS))
+            return w1_codes, w1_scales
+
+        def quantise_w2(u, grouped_tiles):
+            quantise_unit(grouped_tiles, w2_codes, w2_scales, slice(u * ROWS, (u + 1) * ROWS))
 
         def first_matmul(u, w1_codes, w1_scales):
             acc = psum.tile([P, TOKEN_TILES, ROWS], F32, tag="bank", name="acc")
@@ -120,30 +130,22 @@ def tile_crossfusion_pa_kernel(
             nc.vector.tensor_tensor(
                 out=llm[:, :, cols],
                 in0=acc[:],
-                in1=bias_all[:, cols].unsqueeze(1).to_broadcast([P, TOKEN_TILES, ROWS]),
+                in1=b1_all[:, cols].unsqueeze(1).to_broadcast([P, TOKEN_TILES, ROWS]),
                 op=ALU.add,
             )
+
+        def statistics(u):
             for i in range(TOKEN_TILES):
-                nc.vector.bn_stats(out=stats[:, i, u, :], in_=llm[:, i, cols])
-
-        def quantise_w1(grouped_tiles):
-            w1_codes = w1q.tile([P, PASSES1, ROWS], U32, align_bytes=64, name="w1_codes")
-            w1_scales = w1q.tile([P, PASSES1, ROWS], U8, align_bytes=64, name="w1_scales")
-            quantise_unit(grouped_tiles, w1_codes, w1_scales, slice(0, ROWS))
-            return w1_codes, w1_scales
-
-        def quantise_w2(u, grouped_tiles):
-            quantise_unit(grouped_tiles, w2_codes, w2_scales, slice(u * ROWS, (u + 1) * ROWS))
+                nc.vector.bn_stats(out=stats[:, i, u, :], in_=llm[:, i, u * ROWS : (u + 1) * ROWS])
 
         quantise_unit(transpose_unit(x_raw, PASSES1), x_codes, x_scales, slice(0, TOKENS))
 
-        bias_all = keep.tile([P, 2 * DIM], BF16)
-        for c in range(2 * CHUNKS):
+        for c in range(CHUNKS):
             bank = psum.tile([P, BANK], F32, tag="bank", name="bank")
             nc.tensor.matmul(
-                out=bank[:], lhsT=ones[:], rhs=bias_rows[:, c * BANK : (c + 1) * BANK], start=True, stop=True
+                out=bank[:], lhsT=ones[:], rhs=b1_rows[:, c * BANK : (c + 1) * BANK], start=True, stop=True
             )
-            nc.vector.tensor_copy(out=bias_all[:, c * BANK : (c + 1) * BANK], in_=bank[:])
+            nc.vector.tensor_copy(out=b1_all[:, c * BANK : (c + 1) * BANK], in_=bank[:])
         gb_bank = psum.tile([P, BANK], F32, tag="bank", name="bank")
         nc.tensor.transpose(gb_bank[:, 0:P], gb_rows[:].bitcast(F32), ident[:])
         gb_col = keep.tile([P, 2, UNITS, 2], F32)
@@ -154,14 +156,14 @@ def tile_crossfusion_pa_kernel(
         ready = quantise_w1(transpose_unit(w1_raw[0], PASSES1))
         for u in range(UNITS):
             if u + 1 < UNITS:
-                following = transpose_unit(w1_raw[u + 1], PASSES1)
+                following = quantise_w1(transpose_unit(w1_raw[u + 1], PASSES1))
             else:
-                following = transpose_unit(w2_raw[0], PASSES2)
+                quantise_w2(0, transpose_unit(w2_raw[0], PASSES2))
+            if u > 0:
+                statistics(u - 1)
             first_matmul(u, ready[0], ready[1])
-            if u + 1 < UNITS:
-                ready = quantise_w1(following)
-            else:
-                quantise_w2(0, following)
+            ready = following
+        statistics(UNITS - 1)
         for i in range(TOKEN_TILES):
             nc.sync.dma_start(out=llm_out[i * P : (i + 1) * P, :], in_=llm[:, i, :])
 
@@ -177,11 +179,8 @@ def tile_crossfusion_pa_kernel(
         nc.vector.scalar_tensor_tensor(
             out=offset[:], in0=mean_var[:, :, 0], scalar=-1.0, in1=rstd[:], op0=ALU.mult, op1=ALU.mult
         )
-        quantise_w2(1, w2_grouped)
 
         xhat = keep.tile([P, TOKEN_TILES, UNITS, 2, P], F32)
-        n_codes = keep.tile([P, PASSES2, TOKENS], U32, align_bytes=64)
-        n_scales = keep.tile([P, PASSES2, TOKENS], U8, align_bytes=64)
         for g in range(PASSES2):
             for i in range(TOKEN_TILES):
                 source = llm[:, i, g * K_PASS : (g + 1) * K_PASS].rearrange("t (b p e) -> t b e p", b=2, e=2)
@@ -195,6 +194,12 @@ def tile_crossfusion_pa_kernel(
                     nc.scalar.activation(
                         out=target, in_=source, func=ACT.Identity, scale=rstd[:, i : i + 1], bias=offset[:, i : i + 1]
                     )
+        quantise_w2(1, w2_grouped)
+
+        n_codes = keep.tile([P, PASSES2, TOKENS], U32, align_bytes=64)
+        n_scales = keep.tile([P, PASSES2, TOKENS], U8, align_bytes=64)
+        n_grouped = []
+        for g in range(PASSES2):
             planes = stage.tile([P, PACK, TOKENS], BF16, tag="planes", name="planes", bufs=2)
             for u in range(2):
                 b = 2 * g + u
@@ -203,30 +208,41 @@ def tile_crossfusion_pa_kernel(
                     for i in range(TOKEN_TILES):
                         nc.tensor.transpose(bank[:, e, i * P : (i + 1) * P], xhat[:, i, b, e, :], ident[:])
                 for e in range(2):
-                    nc.scalar.activation(
-                        out=planes[:, 2 * u + e, :], in_=bank[:, e, :], func=ACT.Identity,
-                        scale=gb_col[:, 0, b, e : e + 1], bias=gb_col[:, 1, b, e : e + 1],
-                    )
-            grouped = stage.tile([P, TOKENS * PACK], BF16, align_bytes=64, tag="grouped", name="grouped")
+                    gain = gb_col[:, 0, b, e : e + 1]
+                    shift = gb_col[:, 1, b, e : e + 1]
+                    if u == 0:
+                        nc.scalar.activation(
+                            out=planes[:, 2 * u + e, :], in_=bank[:, e, :], func=ACT.Identity, scale=gain, bias=shift
+                        )
+                    else:
+                        nc.vector.tensor_scalar(
+                            out=planes[:, 2 * u + e, :], in0=bank[:, e, :], scalar1=gain, scalar2=shift,
+                            op0=ALU.mult, op1=ALU.add,
+                        )
+            grouped = stage.tile([P, TOKENS * PACK], BF16, align_bytes=64, tag="n_grouped", name="n_grouped", bufs=3)
             nc.vector.tensor_copy(
                 out=grouped[:].rearrange("p (r t) -> p r t", t=PACK), in_=planes[:].rearrange("p t r -> p r t")
             )
-            w2_grouped = transpose_unit(w2_raw[2 + g], PASSES2)
-            nc.vector.quantize_mx(out=n_codes[:, g, :].bitcast(FP8X4), scales=n_scales[:, g, :], in_=grouped[:])
-            quantise_w2(2 + g, w2_grouped)
-        quantise_w2(5, transpose_unit(w2_raw[5], PASSES2))
+            n_grouped.append(grouped)
+            if g > 0:
+                nc.vector.quantize_mx(
+                    out=n_codes[:, g - 1, :].bitcast(FP8X4), scales=n_scales[:, g - 1, :], in_=n_grouped[g - 1][:]
+                )
+        last = PASSES2 - 1
+        nc.vector.quantize_mx(out=n_codes[:, last, :].bitcast(FP8X4), scales=n_scales[:, last, :], in_=n_grouped[last][:])
+
+        for u in range(2, UNITS):
+            quantise_w2(u, transpose_unit(w2_raw[u], PASSES2))
 
         q_sb = keep.tile([P, TOKEN_TILES, DIM], F32)
-        accs = {}
-        for g in range(PASSES2):
+        for c in range(CHUNKS):
+            cols = slice(c * BANK, (c + 1) * BANK)
             for i in range(TOKEN_TILES):
                 tokens = slice(i * P, (i + 1) * P)
-                for c in range(CHUNKS):
-                    cols = slice(c * BANK, (c + 1) * BANK)
-                    if g == 0:
-                        accs[(i, c)] = psum.tile([P, BANK], F32, tag="bank", name="acc")
+                acc = psum.tile([P, BANK], F32, tag="bank", name="acc")
+                for g in range(PASSES2):
                     nc.tensor.matmul_mx(
-                        out=accs[(i, c)][:],
+                        out=acc[:],
                         lhsT=n_codes[:, g, tokens].bitcast(FP8X4),
                         lhsT_scale=n_scales[:, g, tokens],
                         rhs=w2_codes[:, g, cols].bitcast(FP8X4),
@@ -234,11 +250,5 @@ def tile_crossfusion_pa_kernel(
                         start=(g == 0),
                         stop=(g == PASSES2 - 1),
                     )
-        for i in range(TOKEN_TILES):
-            for c in range(CHUNKS):
-                cols = slice(c * BANK, (c + 1) * BANK)
-                nc.vector.tensor_tensor(
-                    out=q_sb[:, i, cols], in0=accs[(i, c)][:], in1=bias_all[:, DIM + c * BANK : DIM + (c + 1) * BANK],
-                    op=ALU.add,
-                )
+                nc.vector.tensor_tensor(out=q_sb[:, i, cols], in0=acc[:], in1=qb_all[:, cols], op=ALU.add)
                 nc.sync.dma_start(out=q_out[i * P : (i + 1) * P, cols], in_=q_sb[:, i, cols])

@@ -40,7 +40,7 @@ def tile_crossfusion_pa_kernel(
         name="stage", bufs=6
     ) as stage, tc.tile_pool(name="w1q", bufs=3) as w1q, tc.psum_pool(
         name="psum", bufs=8
-    ) as psum, tc.manual_schedule():
+    ) as psum:
 
         def load_unit(rows, width, name):
             raw = keep.tile([P, 2, width], BF16, name=name)

@@ -23,6 +23,7 @@ PASSES2 = DIM // K_PASS
 UNITS = DIM // ROWS
 BANK = 512
 CHUNKS = DIM // BANK
+PSUM_BANKS = 8
 EPS = 1e-5
 
 FLOPS = 2 * TOKENS * K1 * DIM + 2 * TOKENS * DIM * DIM
@@ -39,17 +40,12 @@ def tile_crossfusion_pa_kernel(
     with tc.tile_pool(name="keep", bufs=1) as keep, tc.tile_pool(
         name="stage", bufs=6
     ) as stage, tc.tile_pool(name="w1q", bufs=3) as w1q, tc.psum_pool(
-        name="psum", bufs=8
+        name="psum", bufs=PSUM_BANKS
     ) as psum:
-
-        def load_unit(rows, width, name):
-            raw = keep.tile([P, 2, width], BF16, name=name)
-            nc.sync.dma_start(out=raw[:], in_=rows.rearrange("(r p) k -> p r k", p=P))
-            return raw
 
         b1_rows = keep.tile([P, DIM], BF16)
         nc.vector.memset(b1_rows[:].bitcast(I32), 0)
-        gb_rows = keep.tile([P, 2 * P], BF16)
+        gb_rows = keep.tile([P, ROWS], BF16)
         nc.vector.memset(gb_rows[:].bitcast(I32), 0)
         ones = keep.tile([P, P], BF16)
         nc.vector.memset(ones[:], 1.0)
@@ -60,17 +56,22 @@ def tile_crossfusion_pa_kernel(
         warm = keep.tile([P, 1], F32)
         nc.scalar.activation(out=warm[:], in_=eps[:], func=ACT.Sqrt)
 
-        x_raw = load_unit(x_rows, K1, "x_raw")
+        def load_unit(rows, width, name):
+            raw = keep.tile([P, 2, width], BF16, name=name)
+            nc.sync.dma_start(out=raw[:], in_=rows.rearrange("(r p) k -> p r k", p=P))
+            return raw
+
         nc.sync.dma_start(out=b1_rows[0:1, :], in_=llm_proj_b.rearrange("(o n) -> o n", o=1))
         nc.sync.dma_start(out=gb_rows[0:UNITS, :], in_=kvn_g.rearrange("(b w) -> b w", w=ROWS))
         nc.sync.dma_start(out=gb_rows[UNITS : 2 * UNITS, :], in_=kvn_b.rearrange("(b w) -> b w", w=ROWS))
+        x_raw = load_unit(x_rows, K1, "x_raw")
         w1_raw = [load_unit(llm_proj_w[u * ROWS : (u + 1) * ROWS, :], K1, "w1_raw%d" % u) for u in range(UNITS)]
         w2_raw = [load_unit(q_w[u * ROWS : (u + 1) * ROWS, :], DIM, "w2_raw%d" % u) for u in range(UNITS)]
         qb_all = keep.tile([P, DIM], BF16)
         nc.sync.dma_start(out=qb_all[:], in_=q_b.partition_broadcast(P))
 
         def transpose_unit(raw, passes):
-            grouped_tiles = []
+            banks = []
             for g in range(passes):
                 bank = psum.tile([P, 2, ROWS], F32, tag="bank", name="bank")
                 for u in range(2):
@@ -81,6 +82,12 @@ def tile_crossfusion_pa_kernel(
                             raw[:, r, :].bitcast(F32)[:, first : first + P],
                             ident[:],
                         )
+                banks.append(bank)
+            return banks
+
+        def empty_banks(banks):
+            grouped_tiles = []
+            for bank in banks:
                 grouped = stage.tile([P, ROWS * PACK], BF16, align_bytes=64, tag="grouped", name="grouped")
                 nc.scalar.copy(
                     out=grouped[:].bitcast(F32).rearrange("p (c u) -> p c u", u=2),
@@ -138,8 +145,6 @@ def tile_crossfusion_pa_kernel(
             for i in range(TOKEN_TILES):
                 nc.vector.bn_stats(out=stats[:, i, u, :], in_=llm[:, i, u * ROWS : (u + 1) * ROWS])
 
-        quantise_unit(transpose_unit(x_raw, PASSES1), x_codes, x_scales, slice(0, TOKENS))
-
         for c in range(CHUNKS):
             bank = psum.tile([P, BANK], F32, tag="bank", name="bank")
             nc.tensor.matmul(
@@ -153,12 +158,13 @@ def tile_crossfusion_pa_kernel(
             out=gb_col[:].rearrange("p v b e -> p (v b e)"), in_=gb_bank[:, 0 : 2 * UNITS].bitcast(BF16)
         )
 
-        ready = quantise_w1(transpose_unit(w1_raw[0], PASSES1))
+        quantise_unit(empty_banks(transpose_unit(x_raw, PASSES1)), x_codes, x_scales, slice(0, TOKENS))
+        ready = quantise_w1(empty_banks(transpose_unit(w1_raw[0], PASSES1)))
         for u in range(UNITS):
             if u + 1 < UNITS:
-                following = quantise_w1(transpose_unit(w1_raw[u + 1], PASSES1))
+                following = quantise_w1(empty_banks(transpose_unit(w1_raw[u + 1], PASSES1)))
             else:
-                quantise_w2(0, transpose_unit(w2_raw[0], PASSES2))
+                quantise_w2(0, empty_banks(transpose_unit(w2_raw[0], PASSES2)))
             if u > 0:
                 statistics(u - 1)
             first_matmul(u, ready[0], ready[1])
@@ -167,7 +173,8 @@ def tile_crossfusion_pa_kernel(
         for i in range(TOKEN_TILES):
             nc.sync.dma_start(out=llm_out[i * P : (i + 1) * P, :], in_=llm[:, i, :])
 
-        w2_grouped = transpose_unit(w2_raw[1], PASSES2)
+        w2_grouped = empty_banks(transpose_unit(w2_raw[1], PASSES2))
+        w2_banks = transpose_unit(w2_raw[2], PASSES2)
         mean_var = keep.tile([P, TOKEN_TILES, 2], F32)
         for i in range(TOKEN_TILES):
             nc.vector.bn_aggr(out=mean_var[:, i, :], in_=stats[:, i, :, :].rearrange("p u s -> p (u s)"))
@@ -221,7 +228,8 @@ def tile_crossfusion_pa_kernel(
                         )
             grouped = stage.tile([P, TOKENS * PACK], BF16, align_bytes=64, tag="n_grouped", name="n_grouped", bufs=3)
             nc.vector.tensor_copy(
-                out=grouped[:].rearrange("p (r t) -> p r t", t=PACK), in_=planes[:].rearrange("p t r -> p r t")
+                out=grouped[:].rearrange("p (c i t) -> p c t i", i=4, t=PACK),
+                in_=planes[:].rearrange("p t (c i) -> p c t i", i=4),
             )
             n_grouped.append(grouped)
             if g > 0:
@@ -231,12 +239,17 @@ def tile_crossfusion_pa_kernel(
         last = PASSES2 - 1
         nc.vector.quantize_mx(out=n_codes[:, last, :].bitcast(FP8X4), scales=n_scales[:, last, :], in_=n_grouped[last][:])
 
-        for u in range(2, UNITS):
-            quantise_w2(u, transpose_unit(w2_raw[u], PASSES2))
+        quantise_w2(2, empty_banks(w2_banks))
+        quantise_w2(3, empty_banks(transpose_unit(w2_raw[3], PASSES2)))
 
+        units_ready = 4
         q_sb = keep.tile([P, TOKEN_TILES, DIM], F32)
         for c in range(CHUNKS):
+            u = units_ready + c
+            if u < UNITS:
+                w2_grouped = empty_banks(transpose_unit(w2_raw[u], PASSES2))
             cols = slice(c * BANK, (c + 1) * BANK)
+            accs = []
             for i in range(TOKEN_TILES):
                 tokens = slice(i * P, (i + 1) * P)
                 acc = psum.tile([P, BANK], F32, tag="bank", name="acc")
@@ -250,5 +263,9 @@ def tile_crossfusion_pa_kernel(
                         start=(g == 0),
                         stop=(g == PASSES2 - 1),
                     )
-                nc.vector.tensor_tensor(out=q_sb[:, i, cols], in0=acc[:], in1=qb_all[:, cols], op=ALU.add)
+                accs.append(acc)
+            if u < UNITS:
+                quantise_w2(u, w2_grouped)
+            for i in range(TOKEN_TILES):
+                nc.vector.tensor_tensor(out=q_sb[:, i, cols], in0=accs[i][:], in1=qb_all[:, cols], op=ALU.add)
                 nc.sync.dma_start(out=q_out[i * P : (i + 1) * P, cols], in_=q_sb[:, i, cols])

import concourse.mybir as mybir
from concourse.masks import make_identity

F32 = mybir.dt.float32
BF16 = mybir.dt.bfloat16
U32 = mybir.dt.uint32
U8 = mybir.dt.uint8
I32 = mybir.dt.int32
FP8X4 = mybir.dt.float8_e4m3fn_x4
ALU = mybir.AluOpType
ACT = mybir.ActivationFunctionType

P = 128
PACK = 4
K_PASS = P * PACK
ROWS = 2 * P
TOKENS = 256
TOKEN_TILES = TOKENS // P
K1 = 2048
DIM = 1536
PASSES1 = K1 // K_PASS
PASSES2 = DIM // K_PASS
UNITS = DIM // ROWS
BANK = 512
CHUNKS = DIM // BANK
PSUM_BANKS = 8
EPS = 1e-5

FLOPS = 2 * TOKENS * K1 * DIM + 2 * TOKENS * DIM * DIM


def tile_crossfusion_pa_kernel(
    tc, llm_embed, llm_proj_w, llm_proj_b, kvn_g, kvn_b, q_w, q_b, out_0, out_1
):
    nc = tc.nc
    x_rows = llm_embed.flatten_outer_dims()
    llm_out = out_0.flatten_outer_dims()
    q_out = out_1.flatten_outer_dims()

    with tc.tile_pool(name="keep", bufs=1) as keep, tc.tile_pool(
        name="stage", bufs=6
    ) as stage, tc.tile_pool(name="w1q", bufs=3) as w1q, tc.psum_pool(
        name="psum", bufs=PSUM_BANKS
    ) as psum:

        b1_rows = keep.tile([P, DIM], BF16)
        nc.vector.memset(b1_rows[:].bitcast(I32), 0)
        gb_rows = keep.tile([P, ROWS], BF16)
        nc.vector.memset(gb_rows[:].bitcast(I32), 0)
        ones = keep.tile([P, P], BF16)
        nc.vector.memset(ones[:], 1.0)
        eps = keep.tile([P, 1], F32)
        nc.vector.memset(eps[:], EPS)
        ident = keep.tile([P, P], F32)
        make_identity(nc, ident[:])
        warm = keep.tile([P, 1], F32)
        nc.scalar.activation(out=warm[:], in_=eps[:], func=ACT.Sqrt)

        def load_unit(rows, width, name):
            raw = keep.tile([P, 2, width], BF16, name=name)
            nc.sync.dma_start(out=raw[:], in_=rows.rearrange("(r p) k -> p r k", p=P))
            return raw

        nc.sync.dma_start(out=b1_rows[0:1, :], in_=llm_proj_b.rearrange("(o n) -> o n", o=1))
        nc.sync.dma_start(out=gb_rows[0:UNITS, :], in_=kvn_g.rearrange("(b w) -> b w", w=ROWS))
        nc.sync.dma_start(out=gb_rows[UNITS : 2 * UNITS, :], in_=kvn_b.rearrange("(b w) -> b w", w=ROWS))
        x_raw = load_unit(x_rows, K1, "x_raw")
        w1_raw = [load_unit(llm_proj_w[u * ROWS : (u + 1) * ROWS, :], K1, "w1_raw%d" % u) for u in range(UNITS)]
        w2_raw = [load_unit(q_w[u * ROWS : (u + 1) * ROWS, :], DIM, "w2_raw%d" % u) for u in range(UNITS)]
        qb_all = keep.tile([P, DIM], BF16)
        nc.sync.dma_start(out=qb_all[:], in_=q_b.partition_broadcast(P))

        def transpose_unit(raw, passes):
            banks = []
            for g in range(passes):
                bank = psum.tile([P, 2, ROWS], F32, tag="bank", name="bank")
                for u in range(2):
                    first = (2 * g + u) * P
                    for r in range(2):
                        nc.tensor.transpose(
                            bank[:, u, r * P : (r + 1) * P],
                            raw[:, r, :].bitcast(F32)[:, first : first + P],
                            ident[:],
                        )
                banks.append(bank)
            return banks

        def empty_banks(banks):
            grouped_tiles = []
            for bank in banks:
                grouped = stage.tile([P, ROWS * PACK], BF16, align_bytes=64, tag="grouped", name="grouped")
                nc.scalar.copy(
                    out=grouped[:].bitcast(F32).rearrange("p (c u) -> p c u", u=2),
                    in_=bank[:].rearrange("p u c -> p c u"),
                )
                grouped_tiles.append(grouped)
            return grouped_tiles

        def quantise_unit(grouped_tiles, codes, scales, cols):
            for g, grouped in enumerate(grouped_tiles):
                nc.vector.quantize_mx(
                    out=codes[:, g, cols].bitcast(FP8X4), scales=scales[:, g, cols], in_=grouped[:]
                )

        x_codes = keep.tile([P, PASSES1, TOKENS], U32, align_bytes=64)
        x_scales = keep.tile([P, PASSES1, TOKENS], U8, align_bytes=64)
        w2_codes = keep.tile([P, PASSES2, DIM], U32, align_bytes=64)
        w2_scales = keep.tile([P, PASSES2, DIM], U8, align_bytes=64)
        b1_all = keep.tile([P, DIM], BF16)
        llm = keep.tile([P, TOKEN_TILES, DIM], F32)
        stats = keep.tile([P, TOKEN_TILES, UNITS, 6], F32)

        def quantise_w1(grouped_tiles):
            w1_codes = w1q.tile([P, PASSES1, ROWS], U32, align_bytes=64, name="w1_codes")
            w1_scales = w1q.tile([P, PASSES1, ROWS], U8, align_bytes=64, name="w1_scales")
            quantise_unit(grouped_tiles, w1_codes, w1_scales, slice(0, ROWS))
            return w1_codes, w1_scales

        def quantise_w2(u, grouped_tiles):
            quantise_unit(grouped_tiles, w2_codes, w2_scales, slice(u * ROWS, (u + 1) * ROWS))

        def first_matmul(u, w1_codes, w1_scales):
            acc = psum.tile([P, TOKEN_TILES, ROWS], F32, tag="bank", name="acc")
            for i in range(TOKEN_TILES):
                tokens = slice(i * P, (i + 1) * P)
                for g in range(PASSES1):
                    nc.tensor.matmul_mx(
                        out=acc[:, i, :],
                        lhsT=x_codes[:, g, tokens].bitcast(FP8X4),
                        lhsT_scale=x_scales[:, g, tokens],
                        rhs=w1_codes[:, g, :].bitcast(FP8X4),
                        rhs_scale=w1_scales[:, g, :],
                        start=(g == 0),
                        stop=(g == PASSES1 - 1),
                    )
            cols = slice(u * ROWS, (u + 1) * ROWS)
            nc.vector.tensor_tensor(
                out=llm[:, :, cols],
                in0=acc[:],
                in1=b1_all[:, cols].unsqueeze(1).to_broadcast([P, TOKEN_TILES, ROWS]),
                op=ALU.add,
            )

        def statistics(u):
            for i in range(TOKEN_TILES):
                nc.vector.bn_stats(out=stats[:, i, u, :], in_=llm[:, i, u * ROWS : (u + 1) * ROWS])

        for c in range(CHUNKS):
            bank = psum.tile([P, BANK], F32, tag="bank", name="bank")
            nc.tensor.matmul(
                out=bank[:], lhsT=ones[:], rhs=b1_rows[:, c * BANK : (c + 1) * BANK], start=True, stop=True
            )
            nc.vector.tensor_copy(out=b1_all[:, c * BANK : (c + 1) * BANK], in_=bank[:])
        gb_bank = psum.tile([P, BANK], F32, tag="bank", name="bank")
        nc.tensor.transpose(gb_bank[:, 0:P], gb_rows[:].bitcast(F32), ident[:])
        gb_col = keep.tile([P, 2, UNITS, 2], F32)
        nc.vector.tensor_copy(
            out=gb_col[:].rearrange("p v b e -> p (v b e)"), in_=gb_bank[:, 0 : 2 * UNITS].bitcast(BF16)
        )

        quantise_unit(empty_banks(transpose_unit(x_raw, PASSES1)), x_codes, x_scales, slice(0, TOKENS))
        ready = quantise_w1(empty_banks(transpose_unit(w1_raw[0], PASSES1)))
        for u in range(UNITS):
            if u + 1 < UNITS:
                following = quantise_w1(empty_banks(transpose_unit(w1_raw[u + 1], PASSES1)))
            else:
                quantise_w2(0, empty_banks(transpose_unit(w2_raw[0], PASSES2)))
            if u > 0:
                statistics(u - 1)
            first_matmul(u, ready[0], ready[1])
            ready = following
        statistics(UNITS - 1)
        for i in range(TOKEN_TILES):
            nc.sync.dma_start(out=llm_out[i * P : (i + 1) * P, :], in_=llm[:, i, :])

        w2_grouped = empty_banks(transpose_unit(w2_raw[1], PASSES2))
        w2_banks = transpose_unit(w2_raw[2], PASSES2)
        mean_var = keep.tile([P, TOKEN_TILES, 2], F32)
        for i in range(TOKEN_TILES):
            nc.vector.bn_aggr(out=mean_var[:, i, :], in_=stats[:, i, :, :].rearrange("p u s -> p (u s)"))
        std = keep.tile([P, TOKEN_TILES], F32)
        nc.scalar.activation(out=std[:], in_=mean_var[:, :, 1], func=ACT.Sqrt, bias=eps[:, 0:1], scale=1.0)
        rstd = keep.tile([P, TOKEN_TILES], F32)
        nc.vector.reciprocal(out=rstd[:], in_=std[:])
        offset = keep.tile([P, TOKEN_TILES], F32)
        nc.vector.scalar_tensor_tensor(
            out=offset[:], in0=mean_var[:, :, 0], scalar=-1.0, in1=rstd[:], op0=ALU.mult, op1=ALU.mult
        )

        xhat = keep.tile([P, TOKEN_TILES, UNITS, 2, P], F32)
        for g in range(PASSES2):
            for i in range(TOKEN_TILES):
                source = llm[:, i, g * K_PASS : (g + 1) * K_PASS].rearrange("t (b p e) -> t b e p", b=2, e=2)
                target = xhat[:, i, 2 * g : 2 * g + 2, :, :]
                if i == 0:
                    nc.vector.tensor_scalar(
                        out=target, in0=source, scalar1=rstd[:, i : i + 1], scalar2=offset[:, i : i + 1],
                        op0=ALU.mult, op1=ALU.add,
                    )
                else:
                    nc.scalar.activation(
                        out=target, in_=source, func=ACT.Identity, scale=rstd[:, i : i + 1], bias=offset[:, i : i + 1]
                    )
        quantise_w2(1, w2_grouped)

        n_codes = keep.tile([P, PASSES2, TOKENS], U32, align_bytes=64)
        n_scales = keep.tile([P, PASSES2, TOKENS], U8, align_bytes=64)
        n_grouped = []
        for g in range(PASSES2):
            planes = stage.tile([P, PACK, TOKENS], BF16, tag="planes", name="planes", bufs=2)
            for u in range(2):
                b = 2 * g + u
                bank = psum.tile([P, 2, TOKENS], F32, tag="bank", name="bank")
                for e in range(2):
                    for i in range(TOKEN_TILES):
                        nc.tensor.transpose(bank[:, e, i * P : (i + 1) * P], xhat[:, i, b, e, :], ident[:])
                for e in range(2):
                    gain = gb_col[:, 0, b, e : e + 1]
                    shift = gb_col[:, 1, b, e : e + 1]
                    if u == 0:
                        nc.scalar.activation(
                            out=planes[:, 2 * u + e, :], in_=bank[:, e, :], func=ACT.Identity, scale=gain, bias=shift
                        )
                    else:
                        nc.vector.tensor_scalar(
                            out=planes[:, 2 * u + e, :], in0=bank[:, e, :], scalar1=gain, scalar2=shift,
                            op0=ALU.mult, op1=ALU.add,
                        )
            grouped = stage.tile([P, TOKENS * PACK], BF16, align_bytes=64, tag="n_grouped", name="n_grouped", bufs=3)
            nc.vector.tensor_copy(
                out=grouped[:].rearrange("p (c i t) -> p c t i", i=4, t=PACK),
                in_=planes[:].rearrange("p t (c i) -> p c t i", i=4),
            )
            n_grouped.append(grouped)
            if g > 0:
                nc.vector.quantize_mx(
                    out=n_codes[:, g - 1, :].bitcast(FP8X4), scales=n_scales[:, g - 1, :], in_=n_grouped[g - 1][:]
                )
        last = PASSES2 - 1
        nc.vector.quantize_mx(out=n_codes[:, last, :].bitcast(FP8X4), scales=n_scales[:, last, :], in_=n_grouped[last][:])

        quantise_w2(2, empty_banks(w2_banks))
        quantise_w2(3, empty_banks(transpose_unit(w2_raw[3], PASSES2)))

        units_ready = 4
        q_sb = keep.tile([P, TOKEN_TILES, DIM], F32)
        for c in range(CHUNKS):
            u = units_ready + c
            if u < UNITS:
                w2_grouped = empty_banks(transpose_unit(w2_raw[u], PASSES2))
            cols = slice(c * BANK, (c + 1) * BANK)
            accs = []
            for i in range(TOKEN_TILES):
                tokens = slice(i * P, (i + 1) * P)
                acc = psum.tile([P, BANK], F32, tag="bank", name="acc")
                for g in range(PASSES2):
                    nc.tensor.matmul_mx(
                        out=acc[:],
                        lhsT=n_codes[:, g, tokens].bitcast(FP8X4),
                        lhsT_scale=n_scales[:, g, tokens],
                        rhs=w2_codes[:, g, cols].bitcast(FP8X4),
                        rhs_scale=w2_scales[:, g, cols],
                        start=(g == 0),
                        stop=(g == PASSES2 - 1),
                    )
                accs.append(acc)
            if u < UNITS:
                quantise_w2(u, w2_grouped)
            for i in range(TOKEN_TILES):
                nc.vector.tensor_tensor(out=q_sb[:, i, cols], in0=accs[i][:], in1=qb_all[:, cols], op=ALU.add)
                nc.sync.dma_start(out=q_out[i * P : (i + 1) * P, cols], in_=q_sb[:, i, cols])
